import numpy as np
import ml_dtypes


def mxq(x, axis, fmt="e4m3"):
    dtype, down = {"e4m3": (ml_dtypes.float8_e4m3fn, 7), "e5m2": (ml_dtypes.float8_e5m2, 14)}[fmt]
    v = np.moveaxis(np.asarray(x, np.float32).astype(ml_dtypes.bfloat16).astype(np.float64), axis, -1)
    blocks = v.reshape(v.shape[:-1] + (-1, 32))
    amax = np.abs(blocks).max(-1, keepdims=True)
    byte = np.maximum(np.where(amax > 0, np.frexp(amax)[1] - 1 + 127, 0) - down, 1)
    scale = np.exp2(byte - 127.0)
    codes = (blocks / scale).astype(np.float32).astype(dtype).astype(np.float64)
    return np.moveaxis((codes * scale).reshape(v.shape), -1, axis)


WIDE = False


def mx_kscale(k):
    if not WIDE:
        return np.ones(k)
    levels = np.array([10, -10, 5, -5, 0])
    if k % 512:
        return np.exp2(np.random.permutation(np.resize(levels, k // 32))).repeat(32)
    a = np.empty((k // 512, 16))
    for p in range(k // 512):
        a[p, :8] = np.random.permutation(np.resize(levels, 8))
        for g in range(8):
            far = levels[np.abs(levels - a[p, g]) >= 10]
            a[p, g + 8] = far[np.random.randint(len(far))]
    return np.exp2(a.ravel()).repeat(32)


BF16 = ml_dtypes.bfloat16


def bf(x):
    return np.asarray(x, np.float32).astype(BF16)


def f64(x):
    return np.asarray(x).astype(np.float64)


B, N, NIN, CTX, H, NOUT = 2, 512, 512, 3, 1024, 2
F = NIN * CTX


def shift_down(y, d):
    return np.pad(y[:, :-d, :], ((0, 0), (d, 0), (0, 0)))


def shift_up(y, d):
    return np.pad(y[:, d:, :], ((0, 0), (0, d), (0, 0)))


def context_linear(xq, w, shifts):
    y = xq @ mxq(w[:, :NIN].T, 0, "e4m3")
    c = 1
    for d in range(1, CTX // 2 + 1):
        for shift in shifts:
            y = y + shift(xq @ mxq(w[:, c * NIN:(c + 1) * NIN].T, 0, "e4m3"), d)
            c += 1
    return y


def setup_inputs():
    s, u = mx_kscale(NIN), mx_kscale(H)
    return {"x_l": bf(np.random.standard_normal((B, N, NIN)) * s),
            "W_l": bf(np.random.standard_normal((H, F)) / np.sqrt(F) / np.tile(s, CTX) * u[:, None]),
            "b_l": bf(np.random.standard_normal(H) * 0.3 * u),
            "W_bil": bf(np.random.standard_normal((NOUT, H, H)) * 0.2 / np.sqrt(H) / u[None, :, None])}


def reference(x_l, W_l, b_l, W_bil):
    xq = mxq(f64(x_l), 2, "e4m3")
    hl = np.maximum(context_linear(xq, f64(W_l), (shift_down, shift_up)) + f64(b_l), 0.0)
    wb = f64(W_bil).transpose(1, 0, 2).reshape(H, NOUT * H)
    t = mxq(hl, 2, "e4m3") @ mxq(wb, 0, "e4m3")
    return t.reshape(B, N, NOUT, H)

@@ -1,0 +1,224 @@
+from contextlib import ExitStack
+
+import concourse.mybir as mybir
+from concourse.masks import make_identity
+
+F32 = mybir.dt.float32
+BF16 = mybir.dt.bfloat16
+U32 = mybir.dt.uint32
+U8 = mybir.dt.uint8
+FP8X4 = mybir.dt.float8_e4m3fn_x4
+RELU = mybir.ActivationFunctionType.Relu
+
+P = 128
+PACK = 4
+K_PASS = P * PACK
+BANK = 512
+
+SEQS, POSITIONS, FEATURES, WINDOW, HIDDEN, MAPS = 2, 512, 512, 3, 1024, 2
+H_PASSES = HIDDEN // K_PASS
+H_TILES = HIDDEN // P
+LANES = POSITIONS // P
+X_BLOCKS = LANES + 2
+X_COLS = X_BLOCKS * P
+WORDS = FEATURES // 2
+ROUNDS = MAPS * HIDDEN // BANK
+TOKEN_TILES = SEQS * LANES
+SHIFTS = (0, -1, 1)
+PIECE_LAG = 1
+
+FLOPS = 2 * SEQS * POSITIONS * HIDDEN * (WINDOW * FEATURES + MAPS * HIDDEN)
+
+
+def tile_bilinearpairedlayer_pa_kernel(tc, x_l, W_l, b_l, W_bil, out):
+    nc = tc.nc
+    with ExitStack() as ctx:
+        ctx.enter_context(tc.manual_schedule())
+        keep = ctx.enter_context(tc.tile_pool(name="keep", bufs=1))
+        w_stage = ctx.enter_context(tc.tile_pool(name="w_stage", bufs=4))
+        h_stage = ctx.enter_context(tc.tile_pool(name="h_stage", bufs=3))
+        b_stage = ctx.enter_context(tc.tile_pool(name="b_stage", bufs=3))
+        o_stage = ctx.enter_context(tc.tile_pool(name="o_stage", bufs=8))
+        psum = ctx.enter_context(tc.psum_pool(name="psum", bufs=8))
+
+        wl_view = W_l.rearrange("(g p tp t2) f -> g tp p (t2 f)", g=H_PASSES, p=P, tp=2, t2=2)
+        x_raw = []
+        wl_raw = {}
+        for g in range(H_PASSES):
+            x_tile = keep.tile([P, LANES * FEATURES], BF16, name="x_raw%d" % g)
+            nc.sync.dma_start(out=x_tile[:], in_=x_l[g].rearrange("(a s) f -> a (s f)", s=LANES))
+            x_raw.append(x_tile)
+            for tp in range(2):
+                wl_tile = keep.tile([P, 2 * WINDOW * FEATURES], BF16, name="wl_raw%d%d" % (g, tp))
+                nc.sync.dma_start(out=wl_tile[:], in_=wl_view[g, tp])
+                wl_raw[(g, tp)] = wl_tile
+            if g == 0:
+                bias_bf = keep.tile([P, H_TILES], BF16, name="bias_bf")
+                nc.sync.dma_start(
+                    out=bias_bf[:].rearrange("p (g t) -> p g t", g=H_PASSES),
+                    in_=b_l.rearrange("(g p t) -> p g t", g=H_PASSES, p=P, t=PACK),
+                )
+
+        wb_raw = {}
+        for k in range(MAPS):
+            for g in range(H_PASSES):
+                wb_tile = keep.tile([P, PACK, HIDDEN], BF16, name="wb_raw%d%d" % (k, g))
+                nc.sync.dma_start(
+                    out=wb_tile[:],
+                    in_=W_bil[k, g * K_PASS : (g + 1) * K_PASS, :].rearrange("(p t) n -> p t n", t=PACK),
+                )
+                wb_raw[(k, g)] = wb_tile
+
+        ident = keep.tile([P, P], F32, name="ident")
+        make_identity(nc, ident[:])
+
+        x_grouped = keep.tile([P, SEQS * X_COLS * PACK], BF16, name="x_grouped", align_bytes=64)
+        x_codes = keep.tile([P, SEQS, X_COLS], U32, name="x_codes", align_bytes=64)
+        x_scales = keep.tile([P, SEQS, X_COLS], U8, name="x_scales", align_bytes=64)
+        wl_codes = keep.tile([P, WINDOW, HIDDEN], U32, name="wl_codes", align_bytes=64)
+        wl_scales = keep.tile([P, WINDOW, HIDDEN], U8, name="wl_scales", align_bytes=64)
+        hl_codes = keep.tile([P, H_PASSES, SEQS * POSITIONS], U32, name="hl_codes", align_bytes=64)
+        hl_scales = keep.tile([P, H_PASSES, SEQS * POSITIONS], U8, name="hl_scales", align_bytes=64)
+        wb_codes = keep.tile([P, ROUNDS, H_PASSES, BANK], U32, name="wb_codes", align_bytes=64)
+        wb_scales = keep.tile([P, ROUNDS, H_PASSES, BANK], U8, name="wb_scales", align_bytes=64)
+        bias = keep.tile([P, H_TILES], F32, name="bias")
+
+        def transpose_four(words, first_words):
+            bank = psum.tile([P, BANK], F32, tag="bank", name="bank")
+            for i, first in enumerate(first_words):
+                nc.tensor.transpose(bank[:, i * P : (i + 1) * P], words[:, first : first + 2 * P - 1 : 2], ident[:])
+            return bank[:].rearrange("p (r u a) -> p r a u", r=2, u=2, a=P)
+
+        x_words = x_grouped[:].bitcast(F32).rearrange(
+            "p (b j a u) -> p b j a u", b=SEQS, j=X_BLOCKS, a=P, u=2
+        )
+        x_values = x_grouped[:].rearrange("p (b j a t) -> p b j a t", b=SEQS, j=X_BLOCKS, a=P, t=PACK)
+
+        def prepare_x(b):
+            raw_words = x_raw[b][:].bitcast(F32)
+            nc.vector.memset(x_values[:, b, 0, 0, :], 0.0)
+            nc.vector.memset(x_values[:, b, LANES + 1, P - 1, :], 0.0)
+            for sp in range(LANES // 2):
+                firsts = [(2 * sp + r) * WORDS + u for r in range(2) for u in range(2)]
+                turned = transpose_four(raw_words, firsts)
+                nc.scalar.copy(out=x_words[:, b, 1 + 2 * sp : 3 + 2 * sp, :, :], in_=turned)
+            nc.vector.tensor_copy(out=x_values[:, b, LANES + 1, 0 : P - 1, :], in_=x_values[:, b, 1, 1:P, :])
+            nc.vector.tensor_copy(out=x_values[:, b, 0, 1:P, :], in_=x_values[:, b, LANES, 0 : P - 1, :])
+            for first, cols in ((4 * P, 2 * P), (0, 4 * P)):
+                start = (b * X_COLS + first) * PACK
+                nc.vector.quantize_mx(
+                    out=x_codes[:, b, first : first + cols].bitcast(FP8X4),
+                    scales=x_scales[:, b, first : first + cols],
+                    in_=x_grouped[:, start : start + cols * PACK],
+                )
+
+        def prepare_w_l(g):
+            for tp in range(2):
+                raw_words = wl_raw[(g, tp)][:].bitcast(F32)
+                for c in range(WINDOW):
+                    firsts = [(r * WINDOW + c) * WORDS + u for r in range(2) for u in range(2)]
+                    turned = transpose_four(raw_words, firsts)
+                    w_grouped = w_stage.tile([P, 2 * P * PACK], BF16, name="w_grouped", align_bytes=64)
+                    nc.scalar.copy(
+                        out=w_grouped[:].bitcast(F32).rearrange("p (r a u) -> p r a u", r=2, a=P, u=2),
+                        in_=turned,
+                    )
+                    cols = slice((2 * g + tp) * 2 * P, (2 * g + tp + 1) * 2 * P)
+                    nc.vector.quantize_mx(
+                        out=wl_codes[:, c, cols].bitcast(FP8X4),
+                        scales=wl_scales[:, c, cols],
+                        in_=w_grouped[:],
+                    )
+
+        def regroup(grouped, rows):
+            nc.vector.tensor_copy(
+                out=grouped.rearrange("p (c i) t -> p c t i", i=4),
+                in_=rows.rearrange("p t (c i) -> p c t i", i=4),
+            )
+
+        def regroup_w_bil(rnd, g):
+            k, half = divmod(rnd, HIDDEN // BANK)
+            b_grouped = b_stage.tile([P, BANK, PACK], BF16, name="b_grouped", align_bytes=64)
+            regroup(b_grouped[:], wb_raw[(k, g)][:, :, half * BANK : (half + 1) * BANK])
+            return b_grouped
+
+        def quantise_w_bil(rnd, g, b_grouped):
+            nc.vector.quantize_mx(
+                out=wb_codes[:, rnd, g, :].bitcast(FP8X4),
+                scales=wb_scales[:, rnd, g, :],
+                in_=b_grouped[:].rearrange("p n t -> p (n t)"),
+            )
+
+        def first_matmul(g, b):
+            h_rows = h_stage.tile([P, PACK, POSITIONS], BF16, name="h_rows")
+            for t in range(PACK):
+                h_tile = g * PACK + t
+                acc = psum.tile([P, BANK], F32, tag="bank", name="acc")
+                for c in range(WINDOW):
+                    first = (1 + SHIFTS[c]) * P
+                    nc.tensor.matmul_mx(
+                        out=acc[:],
+                        lhsT=wl_codes[:, c, h_tile * P : (h_tile + 1) * P].bitcast(FP8X4),
+                        lhsT_scale=wl_scales[:, c, h_tile * P : (h_tile + 1) * P],
+                        rhs=x_codes[:, b, first : first + POSITIONS].bitcast(FP8X4),
+                        rhs_scale=x_scales[:, b, first : first + POSITIONS],
+                        start=(c == 0),
+                        stop=(c == WINDOW - 1),
+                    )
+                nc.scalar.activation(
+                    out=h_rows[:, t, :], in_=acc[:], func=RELU, bias=bias[:, h_tile : h_tile + 1], scale=1.0
+                )
+            return h_rows
+
+        def quantise_hidden(g, b, h_rows):
+            piece = g * SEQS + b - PIECE_LAG
+            if piece >= H_PASSES:
+                b_grouped = regroup_w_bil(piece // H_PASSES, piece % H_PASSES)
+            h_grouped = h_stage.tile([P, POSITIONS, PACK], BF16, name="h_grouped", align_bytes=64)
+            regroup(h_grouped[:], h_rows[:])
+            if piece >= H_PASSES:
+                quantise_w_bil(piece // H_PASSES, piece % H_PASSES, b_grouped)
+            nc.vector.quantize_mx(
+                out=hl_codes[:, g, b * POSITIONS : (b + 1) * POSITIONS].bitcast(FP8X4),
+                scales=hl_scales[:, g, b * POSITIONS : (b + 1) * POSITIONS],
+                in_=h_grouped[:].rearrange("p n t -> p (n t)"),
+            )
+
+        prepare_x(0)
+        prepare_w_l(0)
+        nc.vector.tensor_copy(out=bias[:], in_=bias_bf[:])
+        prepare_x(1)
+        quantise_hidden(0, 0, first_matmul(0, 0))
+        prepare_w_l(1)
+        round_0 = [regroup_w_bil(0, g) for g in range(H_PASSES)]
+        for g in range(H_PASSES):
+            quantise_w_bil(0, g, round_0[g])
+        for g, b in ((0, 1), (1, 0), (1, 1)):
+            quantise_hidden(g, b, first_matmul(g, b))
+
+        out_view = out.rearrange("b (a s) k n -> b s a k n", s=LANES)
+        for rnd in range(ROUNDS):
+            k, half = divmod(rnd, HIDDEN // BANK)
+            for b in range(SEQS):
+                piece = H_PASSES * SEQS + rnd * SEQS + b - PIECE_LAG
+                if piece < ROUNDS * H_PASSES:
+                    quantise_w_bil(piece // H_PASSES, piece % H_PASSES, regroup_w_bil(piece // H_PASSES, piece % H_PASSES))
+                for s in range(LANES):
+                    m = b * LANES + s
+                    acc = psum.tile([P, BANK], F32, tag="bank", name="acc")
+                    for g in range(H_PASSES):
+                        nc.tensor.matmul_mx(
+                            out=acc[:],
+                            lhsT=hl_codes[:, g, m * P : (m + 1) * P].bitcast(FP8X4),
+                            lhsT_scale=hl_scales[:, g, m * P : (m + 1) * P],
+                            rhs=wb_codes[:, rnd, g, :].bitcast(FP8X4),
+                            rhs_scale=wb_scales[:, rnd, g, :],
+                            start=(g == 0),
+                            stop=(g == H_PASSES - 1),
+                        )
+                    result = o_stage.tile([P, BANK], F32, name="result")
+                    if piece >= ROUNDS * H_PASSES and s % 2 == 1:
+                        nc.vector.tensor_copy(out=result[:], in_=acc[:])
+                    else:
+                        nc.scalar.copy(out=result[:], in_=acc[:])
+                    nc.sync.dma_start(out=out_view[b, s][:, k, half * BANK : (half + 1) * BANK], in_=result[:])

@@ -25,7 +25,6 @@ WORDS = FEATURES // 2
 ROUNDS = MAPS * HIDDEN // BANK
 TOKEN_TILES = SEQS * LANES
 SHIFTS = (0, -1, 1)
-PIECE_LAG = 1
 
 FLOPS = 2 * SEQS * POSITIONS * HIDDEN * (WINDOW * FEATURES + MAPS * HIDDEN)
 
@@ -44,20 +43,23 @@ def tile_bilinearpairedlayer_pa_kernel(tc, x_l, W_l, b_l, W_bil, out):
         wl_view = W_l.rearrange("(g p tp t2) f -> g tp p (t2 f)", g=H_PASSES, p=P, tp=2, t2=2)
         x_raw = []
         wl_raw = {}
-        for g in range(H_PASSES):
-            x_tile = keep.tile([P, LANES * FEATURES], BF16, name="x_raw%d" % g)
-            nc.sync.dma_start(out=x_tile[:], in_=x_l[g].rearrange("(a s) f -> a (s f)", s=LANES))
+        def load_x(b):
+            x_tile = keep.tile([P, LANES * FEATURES], BF16, name="x_raw%d" % b)
+            nc.sync.dma_start(out=x_tile[:], in_=x_l[b].rearrange("(a s) f -> a (s f)", s=LANES))
             x_raw.append(x_tile)
+
+        bias_bf = keep.tile([P, H_TILES], BF16, name="bias_bf")
+        nc.scalar.dma_start(
+            out=bias_bf[:].rearrange("p (g t) -> p g t", g=H_PASSES),
+            in_=b_l.rearrange("(g p t) -> p g t", g=H_PASSES, p=P, t=PACK),
+        )
+        load_x(0)
+        for g in range(H_PASSES):
             for tp in range(2):
                 wl_tile = keep.tile([P, 2 * WINDOW * FEATURES], BF16, name="wl_raw%d%d" % (g, tp))
                 nc.sync.dma_start(out=wl_tile[:], in_=wl_view[g, tp])
                 wl_raw[(g, tp)] = wl_tile
-            if g == 0:
-                bias_bf = keep.tile([P, H_TILES], BF16, name="bias_bf")
-                nc.sync.dma_start(
-                    out=bias_bf[:].rearrange("p (g t) -> p g t", g=H_PASSES),
-                    in_=b_l.rearrange("(g p t) -> p g t", g=H_PASSES, p=P, t=PACK),
-                )
+        load_x(1)
 
         wb_raw = {}
         for k in range(MAPS):
@@ -112,23 +114,22 @@ def tile_bilinearpairedlayer_pa_kernel(tc, x_l, W_l, b_l, W_bil, out):
                     in_=x_grouped[:, start : start + cols * PACK],
                 )
 
-        def prepare_w_l(g):
-            for tp in range(2):
-                raw_words = wl_raw[(g, tp)][:].bitcast(F32)
-                for c in range(WINDOW):
-                    firsts = [(r * WINDOW + c) * WORDS + u for r in range(2) for u in range(2)]
-                    turned = transpose_four(raw_words, firsts)
-                    w_grouped = w_stage.tile([P, 2 * P * PACK], BF16, name="w_grouped", align_bytes=64)
-                    nc.scalar.copy(
-                        out=w_grouped[:].bitcast(F32).rearrange("p (r a u) -> p r a u", r=2, a=P, u=2),
-                        in_=turned,
-                    )
-                    cols = slice((2 * g + tp) * 2 * P, (2 * g + tp + 1) * 2 * P)
-                    nc.vector.quantize_mx(
-                        out=wl_codes[:, c, cols].bitcast(FP8X4),
-                        scales=wl_scales[:, c, cols],
-                        in_=w_grouped[:],
-                    )
+        def prepare_w_l(g, tp):
+            raw_words = wl_raw[(g, tp)][:].bitcast(F32)
+            for c in range(WINDOW):
+                firsts = [(r * WINDOW + c) * WORDS + u for r in range(2) for u in range(2)]
+                turned = transpose_four(raw_words, firsts)
+                w_grouped = w_stage.tile([P, 2 * P * PACK], BF16, name="w_grouped", align_bytes=64)
+                nc.scalar.copy(
+                    out=w_grouped[:].bitcast(F32).rearrange("p (r a u) -> p r a u", r=2, a=P, u=2),
+                    in_=turned,
+                )
+                cols = slice((2 * g + tp) * 2 * P, (2 * g + tp + 1) * 2 * P)
+                nc.vector.quantize_mx(
+                    out=wl_codes[:, c, cols].bitcast(FP8X4),
+                    scales=wl_scales[:, c, cols],
+                    in_=w_grouped[:],
+                )
 
         def regroup(grouped, rows):
             nc.vector.tensor_copy(
@@ -149,9 +150,8 @@ def tile_bilinearpairedlayer_pa_kernel(tc, x_l, W_l, b_l, W_bil, out):
                 in_=b_grouped[:].rearrange("p n t -> p (n t)"),
             )
 
-        def first_matmul(g, b):
-            h_rows = h_stage.tile([P, PACK, POSITIONS], BF16, name="h_rows")
-            for t in range(PACK):
+        def first_matmul(h_rows, g, b, ts):
+            for t in ts:
                 h_tile = g * PACK + t
                 acc = psum.tile([P, BANK], F32, tag="bank", name="acc")
                 for c in range(WINDOW):
@@ -168,57 +168,93 @@ def tile_bilinearpairedlayer_pa_kernel(tc, x_l, W_l, b_l, W_bil, out):
                 nc.scalar.activation(
                     out=h_rows[:, t, :], in_=acc[:], func=RELU, bias=bias[:, h_tile : h_tile + 1], scale=1.0
                 )
+
+        def new_hidden_rows():
+            h_rows = h_stage.tile([P, PACK, POSITIONS], BF16, name="h_rows")
             return h_rows
 
-        def quantise_hidden(g, b, h_rows):
-            piece = g * SEQS + b - PIECE_LAG
-            if piece >= H_PASSES:
-                b_grouped = regroup_w_bil(piece // H_PASSES, piece % H_PASSES)
+        def regroup_hidden(h_rows):
             h_grouped = h_stage.tile([P, POSITIONS, PACK], BF16, name="h_grouped", align_bytes=64)
             regroup(h_grouped[:], h_rows[:])
-            if piece >= H_PASSES:
-                quantise_w_bil(piece // H_PASSES, piece % H_PASSES, b_grouped)
+            return h_grouped
+
+        def quantise_hidden(g, b, h_grouped):
             nc.vector.quantize_mx(
                 out=hl_codes[:, g, b * POSITIONS : (b + 1) * POSITIONS].bitcast(FP8X4),
                 scales=hl_scales[:, g, b * POSITIONS : (b + 1) * POSITIONS],
                 in_=h_grouped[:].rearrange("p n t -> p (n t)"),
             )
 
-        prepare_x(0)
-        prepare_w_l(0)
-        nc.vector.tensor_copy(out=bias[:], in_=bias_bf[:])
-        prepare_x(1)
-        quantise_hidden(0, 0, first_matmul(0, 0))
-        prepare_w_l(1)
-        round_0 = [regroup_w_bil(0, g) for g in range(H_PASSES)]
-        for g in range(H_PASSES):
-            quantise_w_bil(0, g, round_0[g])
-        for g, b in ((0, 1), (1, 0), (1, 1)):
-            quantise_hidden(g, b, first_matmul(g, b))
-
         out_view = out.rearrange("b (a s) k n -> b s a k n", s=LANES)
-        for rnd in range(ROUNDS):
+
+        def second_matmul(rnd, b, vector_lanes=()):
             k, half = divmod(rnd, HIDDEN // BANK)
-            for b in range(SEQS):
-                piece = H_PASSES * SEQS + rnd * SEQS + b - PIECE_LAG
-                if piece < ROUNDS * H_PASSES:
-                    quantise_w_bil(piece // H_PASSES, piece % H_PASSES, regroup_w_bil(piece // H_PASSES, piece % H_PASSES))
-                for s in range(LANES):
-                    m = b * LANES + s
-                    acc = psum.tile([P, BANK], F32, tag="bank", name="acc")
-                    for g in range(H_PASSES):
-                        nc.tensor.matmul_mx(
-                            out=acc[:],
-                            lhsT=hl_codes[:, g, m * P : (m + 1) * P].bitcast(FP8X4),
-                            lhsT_scale=hl_scales[:, g, m * P : (m + 1) * P],
-                            rhs=wb_codes[:, rnd, g, :].bitcast(FP8X4),
-                            rhs_scale=wb_scales[:, rnd, g, :],
-                            start=(g == 0),
-                            stop=(g == H_PASSES - 1),
-                        )
-                    result = o_stage.tile([P, BANK], F32, name="result")
-                    if piece >= ROUNDS * H_PASSES and s % 2 == 1:
-                        nc.vector.tensor_copy(out=result[:], in_=acc[:])
-                    else:
-                        nc.scalar.copy(out=result[:], in_=acc[:])
-                    nc.sync.dma_start(out=out_view[b, s][:, k, half * BANK : (half + 1) * BANK], in_=result[:])
+            for s in range(LANES):
+                m = b * LANES + s
+                acc = psum.tile([P, BANK], F32, tag="bank", name="acc")
+                for g in range(H_PASSES):
+                    nc.tensor.matmul_mx(
+                        out=acc[:],
+                        lhsT=hl_codes[:, g, m * P : (m + 1) * P].bitcast(FP8X4),
+                        lhsT_scale=hl_scales[:, g, m * P : (m + 1) * P],
+                        rhs=wb_codes[:, rnd, g, :].bitcast(FP8X4),
+                        rhs_scale=wb_scales[:, rnd, g, :],
+                        start=(g == 0),
+                        stop=(g == H_PASSES - 1),
+                    )
+                result = o_stage.tile([P, BANK], F32, name="result")
+                if s in vector_lanes:
+                    nc.vector.tensor_copy(out=result[:], in_=acc[:])
+                else:
+                    nc.scalar.copy(out=result[:], in_=acc[:])
+                nc.sync.dma_start(out=out_view[b, s][:, k, half * BANK : (half + 1) * BANK], in_=result[:])
+
+        prepare_x(0)
+        prepare_w_l(0, 0)
+        nc.vector.tensor_copy(out=bias[:], in_=bias_bf[:])
+        prepare_w_l(0, 1)
+        h00 = new_hidden_rows()
+        first_matmul(h00, 0, 0, (0, 1))
+        prepare_w_l(1, 0)
+        first_matmul(h00, 0, 0, (2, 3))
+        prepare_w_l(1, 1)
+        h10 = new_hidden_rows()
+        first_matmul(h10, 1, 0, (0, 1))
+        h00_grouped = regroup_hidden(h00)
+        piece = regroup_w_bil(0, 0)
+        quantise_hidden(0, 0, h00_grouped)
+        quantise_w_bil(0, 0, piece)
+        prepare_x(1)
+        first_matmul(h10, 1, 0, (2, 3))
+        h01 = new_hidden_rows()
+        first_matmul(h01, 0, 1, (0, 1, 2, 3))
+        piece = regroup_w_bil(0, 1)
+        h10_grouped = regroup_hidden(h10)
+        quantise_w_bil(0, 1, piece)
+        quantise_hidden(1, 0, h10_grouped)
+        second_matmul(0, 0)
+        h11 = new_hidden_rows()
+        first_matmul(h11, 1, 1, (0, 1, 2, 3))
+        piece = regroup_w_bil(1, 0)
+        h01_grouped = regroup_hidden(h01)
+        quantise_w_bil(1, 0, piece)
+        piece = regroup_w_bil(1, 1)
+        quantise_hidden(0, 1, h01_grouped)
+        quantise_w_bil(1, 1, piece)
+        second_matmul(1, 0)
+        h11_grouped = regroup_hidden(h11)
+        piece = regroup_w_bil(2, 0)
+        quantise_hidden(1, 1, h11_grouped)
+        quantise_w_bil(2, 0, piece)
+        second_matmul(0, 1)
+        piece = regroup_w_bil(2, 1)
+        piece2 = regroup_w_bil(3, 0)
+        quantise_w_bil(2, 1, piece)
+        quantise_w_bil(3, 0, piece2)
+        second_matmul(1, 1)
+        second_matmul(2, 0)
+        piece = regroup_w_bil(3, 1)
+        quantise_w_bil(3, 1, piece)
+        second_matmul(2, 1, (0, 2))
+        second_matmul(3, 0, (0, 2))
+        second_matmul(3, 1, (0, 2))

@@ -34,43 +34,56 @@ def tile_bilinearpairedlayer_pa_kernel(tc, x_l, W_l, b_l, W_bil, out):
     with ExitStack() as ctx:
         ctx.enter_context(tc.manual_schedule())
         keep = ctx.enter_context(tc.tile_pool(name="keep", bufs=1))
-        w_stage = ctx.enter_context(tc.tile_pool(name="w_stage", bufs=4))
+        w_stage = ctx.enter_context(tc.tile_pool(name="w_stage", bufs=8))
         h_stage = ctx.enter_context(tc.tile_pool(name="h_stage", bufs=3))
-        b_stage = ctx.enter_context(tc.tile_pool(name="b_stage", bufs=3))
+        b_stage = ctx.enter_context(tc.tile_pool(name="b_stage", bufs=4))
         o_stage = ctx.enter_context(tc.tile_pool(name="o_stage", bufs=8))
         psum = ctx.enter_context(tc.psum_pool(name="psum", bufs=8))
 
-        wl_view = W_l.rearrange("(g p tp t2) f -> g tp p (t2 f)", g=H_PASSES, p=P, tp=2, t2=2)
-        x_raw = []
+        wl_view = W_l.rearrange("(g p tp t2) f -> g tp p t2 f", g=H_PASSES, p=P, tp=2, t2=2)
+        x_raw = {}
         wl_raw = {}
-        def load_x(b):
+        wb_raw = {}
+
+        def load_x(b, parts=1):
             x_tile = keep.tile([P, LANES * FEATURES], BF16, name="x_raw%d" % b)
-            nc.sync.dma_start(out=x_tile[:], in_=x_l[b].rearrange("(a s) f -> a (s f)", s=LANES))
-            x_raw.append(x_tile)
+            view = x_l[b].rearrange("(a s) f -> a (s f)", s=LANES)
+            n = LANES * FEATURES // parts
+            for i in range(parts):
+                nc.sync.dma_start(out=x_tile[:, i * n : (i + 1) * n], in_=view[:, i * n : (i + 1) * n])
+            x_raw[b] = x_tile
 
         bias_bf = keep.tile([P, H_TILES], BF16, name="bias_bf")
         nc.scalar.dma_start(
             out=bias_bf[:].rearrange("p (g t) -> p g t", g=H_PASSES),
             in_=b_l.rearrange("(g p t) -> p g t", g=H_PASSES, p=P, t=PACK),
         )
-        load_x(0)
-        for g in range(H_PASSES):
-            for tp in range(2):
-                wl_tile = keep.tile([P, 2 * WINDOW * FEATURES], BF16, name="wl_raw%d%d" % (g, tp))
-                nc.sync.dma_start(out=wl_tile[:], in_=wl_view[g, tp])
-                wl_raw[(g, tp)] = wl_tile
+
+        def load_w_l(g, tp, cuts=(0, WINDOW)):
+            wl_tile = keep.tile([P, 2, WINDOW * FEATURES], BF16, name="wl_raw%d%d" % (g, tp))
+            for first, last in zip(cuts, cuts[1:]):
+                cols = slice(first * FEATURES, last * FEATURES)
+                nc.sync.dma_start(out=wl_tile[:, :, cols], in_=wl_view[g, tp][:, :, cols])
+            wl_raw[(g, tp)] = wl_tile
+
+        def load_w_bil(k, g):
+            wb_tile = keep.tile([P, PACK, HIDDEN], BF16, name="wb_raw%d%d" % (k, g))
+            nc.sync.dma_start(
+                out=wb_tile[:],
+                in_=W_bil[k, g * K_PASS : (g + 1) * K_PASS, :].rearrange("(p t) n -> p t n", t=PACK),
+            )
+            wb_raw[(k, g)] = wb_tile
+
+        load_x(0, 2)
+        load_w_l(0, 0, (0, 1, 3))
+        load_w_l(0, 1)
+        load_w_bil(0, 0)
+        load_w_l(1, 0)
+        load_w_l(1, 1)
         load_x(1)
-
-        wb_raw = {}
-        for k in range(MAPS):
-            for g in range(H_PASSES):
-                wb_tile = keep.tile([P, PACK, HIDDEN], BF16, name="wb_raw%d%d" % (k, g))
-                nc.sync.dma_start(
-                    out=wb_tile[:],
-                    in_=W_bil[k, g * K_PASS : (g + 1) * K_PASS, :].rearrange("(p t) n -> p t n", t=PACK),
-                )
-                wb_raw[(k, g)] = wb_tile
-
+        load_w_bil(0, 1)
+        load_w_bil(1, 0)
+        load_w_bil(1, 1)
         ident = keep.tile([P, P], F32, name="ident")
         make_identity(nc, ident[:])
 
@@ -96,17 +109,21 @@ def tile_bilinearpairedlayer_pa_kernel(tc, x_l, W_l, b_l, W_bil, out):
         )
         x_values = x_grouped[:].rearrange("p (b j a t) -> p b j a t", b=SEQS, j=X_BLOCKS, a=P, t=PACK)
 
-        def prepare_x(b):
-            raw_words = x_raw[b][:].bitcast(F32)
+        for b in range(SEQS):
             nc.vector.memset(x_values[:, b, 0, 0, :], 0.0)
             nc.vector.memset(x_values[:, b, LANES + 1, P - 1, :], 0.0)
+
+        def turn_x(b):
+            raw_words = x_raw[b][:].bitcast(F32)
             for sp in range(LANES // 2):
                 firsts = [(2 * sp + r) * WORDS + u for r in range(2) for u in range(2)]
                 turned = transpose_four(raw_words, firsts)
                 nc.scalar.copy(out=x_words[:, b, 1 + 2 * sp : 3 + 2 * sp, :, :], in_=turned)
+
+        def finish_x(b):
             nc.vector.tensor_copy(out=x_values[:, b, LANES + 1, 0 : P - 1, :], in_=x_values[:, b, 1, 1:P, :])
             nc.vector.tensor_copy(out=x_values[:, b, 0, 1:P, :], in_=x_values[:, b, LANES, 0 : P - 1, :])
-            for first, cols in ((4 * P, 2 * P), (0, 4 * P)):
+            for first, cols in ((P, 4 * P), (0, P), (5 * P, P)):
                 start = (b * X_COLS + first) * PACK
                 nc.vector.quantize_mx(
                     out=x_codes[:, b, first : first + cols].bitcast(FP8X4),
@@ -114,27 +131,47 @@ def tile_bilinearpairedlayer_pa_kernel(tc, x_l, W_l, b_l, W_bil, out):
                     in_=x_grouped[:, start : start + cols * PACK],
                 )
 
-        def prepare_w_l(g, tp):
-            raw_words = wl_raw[(g, tp)][:].bitcast(F32)
+        def turn_w_l(g, tp, evacuate):
+            raw_words = wl_raw[(g, tp)][:].rearrange("p r f -> p (r f)").bitcast(F32)
+            parts = []
             for c in range(WINDOW):
                 firsts = [(r * WINDOW + c) * WORDS + u for r in range(2) for u in range(2)]
                 turned = transpose_four(raw_words, firsts)
                 w_grouped = w_stage.tile([P, 2 * P * PACK], BF16, name="w_grouped", align_bytes=64)
-                nc.scalar.copy(
-                    out=w_grouped[:].bitcast(F32).rearrange("p (r a u) -> p r a u", r=2, a=P, u=2),
-                    in_=turned,
-                )
-                cols = slice((2 * g + tp) * 2 * P, (2 * g + tp + 1) * 2 * P)
+                target = w_grouped[:].bitcast(F32).rearrange("p (r a u) -> p r a u", r=2, a=P, u=2)
+                if c in evacuate:
+                    nc.vector.tensor_copy(out=target, in_=turned)
+                else:
+                    nc.scalar.copy(out=target, in_=turned)
+                parts.append(w_grouped)
+            return parts
+
+        def quantise_w_l(g, tp, parts):
+            cols = slice((2 * g + tp) * 2 * P, (2 * g + tp + 1) * 2 * P)
+            for c in range(WINDOW):
                 nc.vector.quantize_mx(
                     out=wl_codes[:, c, cols].bitcast(FP8X4),
                     scales=wl_scales[:, c, cols],
-                    in_=w_grouped[:],
+                    in_=parts[c][:],
                 )
 
         def regroup(grouped, rows):
             nc.vector.tensor_copy(
                 out=grouped.rearrange("p (c i) t -> p c t i", i=4),
                 in_=rows.rearrange("p t (c i) -> p c t i", i=4),
+            )
+
+        def new_pieces():
+            b_grouped = b_stage.tile([P, BANK, PACK], BF16, name="b_grouped", align_bytes=64)
+            return b_grouped
+
+        def regroup_w_bil_on_scalar(b_grouped, rnd, g, part):
+            k, half = divmod(rnd, HIDDEN // BANK)
+            cols = slice(part * BANK // 2, (part + 1) * BANK // 2)
+            raw = slice(half * BANK + part * BANK // 2, half * BANK + (part + 1) * BANK // 2)
+            nc.scalar.copy(
+                out=b_grouped[:, cols, :].rearrange("p (c i) t -> p c t i", i=4),
+                in_=wb_raw[(k, g)][:, :, raw].rearrange("p t (c i) -> p c t i", i=4),
             )
 
         def regroup_w_bil(rnd, g):
@@ -187,74 +224,100 @@ def tile_bilinearpairedlayer_pa_kernel(tc, x_l, W_l, b_l, W_bil, out):
 
         out_view = out.rearrange("b (a s) k n -> b s a k n", s=LANES)
 
-        def second_matmul(rnd, b, vector_lanes=()):
-            k, half = divmod(rnd, HIDDEN // BANK)
-            for s in range(LANES):
-                m = b * LANES + s
-                acc = psum.tile([P, BANK], F32, tag="bank", name="acc")
-                for g in range(H_PASSES):
-                    nc.tensor.matmul_mx(
-                        out=acc[:],
-                        lhsT=hl_codes[:, g, m * P : (m + 1) * P].bitcast(FP8X4),
-                        lhsT_scale=hl_scales[:, g, m * P : (m + 1) * P],
-                        rhs=wb_codes[:, rnd, g, :].bitcast(FP8X4),
-                        rhs_scale=wb_scales[:, rnd, g, :],
-                        start=(g == 0),
-                        stop=(g == H_PASSES - 1),
-                    )
-                result = o_stage.tile([P, BANK], F32, name="result")
-                if s in vector_lanes:
-                    nc.vector.tensor_copy(out=result[:], in_=acc[:])
-                else:
-                    nc.scalar.copy(out=result[:], in_=acc[:])
-                nc.sync.dma_start(out=out_view[b, s][:, k, half * BANK : (half + 1) * BANK], in_=result[:])
+        def fill_bank(rnd, m):
+            acc = psum.tile([P, BANK], F32, tag="bank", name="acc")
+            for g in range(H_PASSES):
+                nc.tensor.matmul_mx(
+                    out=acc[:],
+                    lhsT=hl_codes[:, g, m * P : (m + 1) * P].bitcast(FP8X4),
+                    lhsT_scale=hl_scales[:, g, m * P : (m + 1) * P],
+                    rhs=wb_codes[:, rnd, g, :].bitcast(FP8X4),
+                    rhs_scale=wb_scales[:, rnd, g, :],
+                    start=(g == 0),
+                    stop=(g == H_PASSES - 1),
+                )
+            return acc
 
-        prepare_x(0)
-        prepare_w_l(0, 0)
+        def second_matmul(rnds, b, lanes, vector_banks, whole=True):
+            k, half = divmod(rnds[0], HIDDEN // BANK)
+            for i, s in enumerate(lanes):
+                m = b * LANES + s
+                result = o_stage.tile([P, 2 * BANK], F32, name="result")
+                for j, rnd in enumerate(rnds):
+                    acc = fill_bank(rnd, m)
+                    target = result[:, j * BANK : (j + 1) * BANK]
+                    if i * len(rnds) + j in vector_banks:
+                        nc.vector.tensor_copy(out=target, in_=acc[:])
+                    else:
+                        nc.scalar.copy(out=target, in_=acc[:])
+                    if not whole:
+                        nc.sync.dma_start(out=out_view[b, s][:, k, (half + j) * BANK : (half + j + 1) * BANK], in_=target)
+                if whole:
+                    nc.sync.dma_start(
+                        out=out_view[b, s][:, k, half * BANK : half * BANK + len(rnds) * BANK],
+                        in_=result[:, 0 : len(rnds) * BANK],
+                    )
+
+        turn_x(0)
+        finish_x(0)
         nc.vector.tensor_copy(out=bias[:], in_=bias_bf[:])
-        prepare_w_l(0, 1)
+        w00 = turn_w_l(0, 0, ())
+        quantise_w_l(0, 0, w00)
+        w01 = turn_w_l(0, 1, ())
+        quantise_w_l(0, 1, w01)
         h00 = new_hidden_rows()
-        first_matmul(h00, 0, 0, (0, 1))
-        prepare_w_l(1, 0)
-        first_matmul(h00, 0, 0, (2, 3))
-        prepare_w_l(1, 1)
-        h10 = new_hidden_rows()
-        first_matmul(h10, 1, 0, (0, 1))
+        first_matmul(h00, 0, 0, (0, 1, 2, 3))
+        b00 = regroup_w_bil(0, 0)
+        b10 = regroup_w_bil(1, 0)
+        quantise_w_bil(0, 0, b00)
+        w10 = turn_w_l(1, 0, ())
+        quantise_w_bil(1, 0, b10)
+        quantise_w_l(1, 0, w10)
         h00_grouped = regroup_hidden(h00)
-        piece = regroup_w_bil(0, 0)
         quantise_hidden(0, 0, h00_grouped)
-        quantise_w_bil(0, 0, piece)
-        prepare_x(1)
-        first_matmul(h10, 1, 0, (2, 3))
+        w11 = turn_w_l(1, 1, ())
+        turn_x(1)
+        quantise_w_l(1, 1, w11)
+        finish_x(1)
+        h10 = new_hidden_rows()
+        first_matmul(h10, 1, 0, (0, 1, 2, 3))
+        b01 = regroup_w_bil(0, 1)
+        b11 = new_pieces()
+        regroup_w_bil_on_scalar(b11, 1, 1, 0)
         h01 = new_hidden_rows()
         first_matmul(h01, 0, 1, (0, 1, 2, 3))
-        piece = regroup_w_bil(0, 1)
         h10_grouped = regroup_hidden(h10)
-        quantise_w_bil(0, 1, piece)
+        quantise_w_bil(0, 1, b01)
         quantise_hidden(1, 0, h10_grouped)
-        second_matmul(0, 0)
+        regroup_w_bil_on_scalar(b11, 1, 1, 1)
+        b20 = regroup_w_bil(2, 0)
         h11 = new_hidden_rows()
         first_matmul(h11, 1, 1, (0, 1, 2, 3))
-        piece = regroup_w_bil(1, 0)
         h01_grouped = regroup_hidden(h01)
-        quantise_w_bil(1, 0, piece)
-        piece = regroup_w_bil(1, 1)
+        quantise_w_bil(1, 1, b11)
+        quantise_w_bil(2, 0, b20)
         quantise_hidden(0, 1, h01_grouped)
-        quantise_w_bil(1, 1, piece)
-        second_matmul(1, 0)
         h11_grouped = regroup_hidden(h11)
-        piece = regroup_w_bil(2, 0)
+        b21 = regroup_w_bil(2, 1)
         quantise_hidden(1, 1, h11_grouped)
-        quantise_w_bil(2, 0, piece)
-        second_matmul(0, 1)
-        piece = regroup_w_bil(2, 1)
-        piece2 = regroup_w_bil(3, 0)
-        quantise_w_bil(2, 1, piece)
-        quantise_w_bil(3, 0, piece2)
-        second_matmul(1, 1)
-        second_matmul(2, 0)
-        piece = regroup_w_bil(3, 1)
-        quantise_w_bil(3, 1, piece)
-        second_matmul(2, 1, (0, 2))
-        second_matmul(3, 0, (0, 2))
-        second_matmul(3, 1, (0, 2))
+        quantise_w_bil(2, 1, b21)
+        second_matmul((0, 1), 0, (0,), ())
+        second_matmul((0, 1), 0, (1,), ())
+        second_matmul((0, 1), 0, (2,), ())
+        second_matmul((0, 1), 0, (3,), ())
+        b30 = regroup_w_bil(3, 0)
+        b31 = regroup_w_bil(3, 1)
+        quantise_w_bil(3, 0, b30)
+        quantise_w_bil(3, 1, b31)
+        second_matmul((0, 1), 1, (0,), ())
+        second_matmul((0, 1), 1, (1,), ())
+        second_matmul((0, 1), 1, (2,), ())
+        second_matmul((0, 1), 1, (3,), ())
+        second_matmul((2, 3), 0, (0,), ())
+        second_matmul((2, 3), 0, (1,), ())
+        second_matmul((2, 3), 0, (2,), ())
+        second_matmul((2, 3), 0, (3,), ())
+        second_matmul((2, 3), 1, (0,), (1,))
+        second_matmul((2, 3), 1, (1,), (1,))
+        second_matmul((2, 3), 1, (2,), (1,))
+        second_matmul((2, 3), 1, (3,), (1,))

@@ -76,7 +76,7 @@ def tile_bilinearpairedlayer_pa_kernel(tc, x_l, W_l, b_l, W_bil, out):
 
         load_x(0, 2)
         load_w_l(0, 0, (0, 1, 3))
-        load_w_l(0, 1)
+        load_w_l(0, 1, (0, 1, 3))
         load_w_bil(0, 0)
         load_w_l(1, 0)
         load_w_l(1, 1)
@@ -108,6 +108,14 @@ def tile_bilinearpairedlayer_pa_kernel(tc, x_l, W_l, b_l, W_bil, out):
             "p (b j a u) -> p b j a u", b=SEQS, j=X_BLOCKS, a=P, u=2
         )
         x_values = x_grouped[:].rearrange("p (b j a t) -> p b j a t", b=SEQS, j=X_BLOCKS, a=P, t=PACK)
+
+        zeros = keep.tile([P, BANK], BF16, name="zeros")
+        nc.vector.memset(zeros[:], 0.0)
+
+        def keep_busy(times):
+            for i in range(times):
+                idle = psum.tile([P, BANK], F32, tag="bank", name="idle")
+                nc.tensor.matmul(out=idle[:], lhsT=zeros[:, 0:P], rhs=zeros[:], start=True, stop=True)
 
         for b in range(SEQS):
             nc.vector.memset(x_values[:, b, 0, 0, :], 0.0)
@@ -258,11 +266,14 @@ def tile_bilinearpairedlayer_pa_kernel(tc, x_l, W_l, b_l, W_bil, out):
                         in_=result[:, 0 : len(rnds) * BANK],
                     )
 
+        keep_busy(5)
         turn_x(0)
         finish_x(0)
         nc.vector.tensor_copy(out=bias[:], in_=bias_bf[:])
+        keep_busy(1)
         w00 = turn_w_l(0, 0, ())
         quantise_w_l(0, 0, w00)
+        keep_busy(1)
         w01 = turn_w_l(0, 1, ())
         quantise_w_l(0, 1, w01)
         h00 = new_hidden_rows()
@@ -275,7 +286,9 @@ def tile_bilinearpairedlayer_pa_kernel(tc, x_l, W_l, b_l, W_bil, out):
         quantise_w_l(1, 0, w10)
         h00_grouped = regroup_hidden(h00)
         quantise_hidden(0, 0, h00_grouped)
+        keep_busy(1)
         w11 = turn_w_l(1, 1, ())
+        keep_busy(1)
         turn_x(1)
         quantise_w_l(1, 1, w11)
         finish_x(1)
@@ -320,4 +333,4 @@ def tile_bilinearpairedlayer_pa_kernel(tc, x_l, W_l, b_l, W_bil, out):
         second_matmul((2, 3), 1, (0,), (1,))
         second_matmul((2, 3), 1, (1,), (1,))
         second_matmul((2, 3), 1, (2,), (1,))
-        second_matmul((2, 3), 1, (3,), (1,))
+        second_matmul((2, 3), 1, (3,), (1,), False)

@@ -96,7 +96,6 @@ def tile_bilinearpairedlayer_pa_kernel(tc, x_l, W_l, b_l, W_bil, out):
         hl_scales = keep.tile([P, H_PASSES, SEQS * POSITIONS], U8, name="hl_scales", align_bytes=64)
         wb_codes = keep.tile([P, ROUNDS, H_PASSES, BANK], U32, name="wb_codes", align_bytes=64)
         wb_scales = keep.tile([P, ROUNDS, H_PASSES, BANK], U8, name="wb_scales", align_bytes=64)
-        bias = keep.tile([P, H_TILES], F32, name="bias")
 
         def transpose_four(words, first_words):
             bank = psum.tile([P, BANK], F32, tag="bank", name="bank")
@@ -108,14 +107,6 @@ def tile_bilinearpairedlayer_pa_kernel(tc, x_l, W_l, b_l, W_bil, out):
             "p (b j a u) -> p b j a u", b=SEQS, j=X_BLOCKS, a=P, u=2
         )
         x_values = x_grouped[:].rearrange("p (b j a t) -> p b j a t", b=SEQS, j=X_BLOCKS, a=P, t=PACK)
-
-        zeros = keep.tile([P, BANK], BF16, name="zeros")
-        nc.vector.memset(zeros[:], 0.0)
-
-        def keep_busy(times):
-            for i in range(times):
-                idle = psum.tile([P, BANK], F32, tag="bank", name="idle")
-                nc.tensor.matmul(out=idle[:], lhsT=zeros[:, 0:P], rhs=zeros[:], start=True, stop=True)
 
         for b in range(SEQS):
             nc.vector.memset(x_values[:, b, 0, 0, :], 0.0)
@@ -211,7 +202,7 @@ def tile_bilinearpairedlayer_pa_kernel(tc, x_l, W_l, b_l, W_bil, out):
                         stop=(c == WINDOW - 1),
                     )
                 nc.scalar.activation(
-                    out=h_rows[:, t, :], in_=acc[:], func=RELU, bias=bias[:, h_tile : h_tile + 1], scale=1.0
+                    out=h_rows[:, t, :], in_=acc[:], func=RELU, bias=bias_bf[:, h_tile : h_tile + 1], scale=1.0
                 )
 
         def new_hidden_rows():
@@ -266,14 +257,10 @@ def tile_bilinearpairedlayer_pa_kernel(tc, x_l, W_l, b_l, W_bil, out):
                         in_=result[:, 0 : len(rnds) * BANK],
                     )
 
-        keep_busy(5)
         turn_x(0)
         finish_x(0)
-        nc.vector.tensor_copy(out=bias[:], in_=bias_bf[:])
-        keep_busy(1)
         w00 = turn_w_l(0, 0, ())
         quantise_w_l(0, 0, w00)
-        keep_busy(1)
         w01 = turn_w_l(0, 1, ())
         quantise_w_l(0, 1, w01)
         h00 = new_hidden_rows()
@@ -286,9 +273,7 @@ def tile_bilinearpairedlayer_pa_kernel(tc, x_l, W_l, b_l, W_bil, out):
         quantise_w_l(1, 0, w10)
         h00_grouped = regroup_hidden(h00)
         quantise_hidden(0, 0, h00_grouped)
-        keep_busy(1)
         w11 = turn_w_l(1, 1, ())
-        keep_busy(1)
         turn_x(1)
         quantise_w_l(1, 1, w11)
         finish_x(1)

@@ -74,9 +74,9 @@ def tile_bilinearpairedlayer_pa_kernel(tc, x_l, W_l, b_l, W_bil, out):
             )
             wb_raw[(k, g)] = wb_tile
 
-        load_x(0, 2)
-        load_w_l(0, 0, (0, 1, 3))
-        load_w_l(0, 1, (0, 1, 3))
+        load_x(0)
+        load_w_l(0, 0)
+        load_w_l(0, 1)
         load_w_bil(0, 0)
         load_w_l(1, 0)
         load_w_l(1, 1)
@@ -318,4 +318,4 @@ def tile_bilinearpairedlayer_pa_kernel(tc, x_l, W_l, b_l, W_bil, out):
         second_matmul((2, 3), 1, (0,), (1,))
         second_matmul((2, 3), 1, (1,), (1,))
         second_matmul((2, 3), 1, (2,), (1,))
-        second_matmul((2, 3), 1, (3,), (1,), False)
+        second_matmul((2, 3), 1, (3,), (1,))

@@ -277,17 +277,17 @@ def tile_bilinearpairedlayer_pa_kernel(tc, x_l, W_l, b_l, W_bil, out):
         turn_x(1)
         quantise_w_l(1, 1, w11)
         finish_x(1)
+        b11 = new_pieces()
+        regroup_w_bil_on_scalar(b11, 1, 1, 0)
         h10 = new_hidden_rows()
         first_matmul(h10, 1, 0, (0, 1, 2, 3))
         b01 = regroup_w_bil(0, 1)
-        b11 = new_pieces()
-        regroup_w_bil_on_scalar(b11, 1, 1, 0)
+        regroup_w_bil_on_scalar(b11, 1, 1, 1)
         h01 = new_hidden_rows()
         first_matmul(h01, 0, 1, (0, 1, 2, 3))
         h10_grouped = regroup_hidden(h10)
         quantise_w_bil(0, 1, b01)
         quantise_hidden(1, 0, h10_grouped)
-        regroup_w_bil_on_scalar(b11, 1, 1, 1)
         b20 = regroup_w_bil(2, 0)
         h11 = new_hidden_rows()
         first_matmul(h11, 1, 1, (0, 1, 2, 3))

@@ -272,8 +272,8 @@ def tile_bilinearpairedlayer_pa_kernel(tc, x_l, W_l, b_l, W_bil, out):
         quantise_w_bil(1, 0, b10)
         quantise_w_l(1, 0, w10)
         h00_grouped = regroup_hidden(h00)
-        quantise_hidden(0, 0, h00_grouped)
         w11 = turn_w_l(1, 1, ())
+        quantise_hidden(0, 0, h00_grouped)
         turn_x(1)
         quantise_w_l(1, 1, w11)
         finish_x(1)
@@ -288,22 +288,24 @@ def tile_bilinearpairedlayer_pa_kernel(tc, x_l, W_l, b_l, W_bil, out):
         h10_grouped = regroup_hidden(h10)
         quantise_w_bil(0, 1, b01)
         quantise_hidden(1, 0, h10_grouped)
+        quantise_w_bil(1, 1, b11)
         b20 = regroup_w_bil(2, 0)
         h11 = new_hidden_rows()
-        first_matmul(h11, 1, 1, (0, 1, 2, 3))
-        h01_grouped = regroup_hidden(h01)
-        quantise_w_bil(1, 1, b11)
-        quantise_w_bil(2, 0, b20)
-        quantise_hidden(0, 1, h01_grouped)
-        h11_grouped = regroup_hidden(h11)
-        b21 = regroup_w_bil(2, 1)
-        quantise_hidden(1, 1, h11_grouped)
-        quantise_w_bil(2, 1, b21)
+        first_matmul(h11, 1, 1, (0, 1))
         second_matmul((0, 1), 0, (0,), ())
         second_matmul((0, 1), 0, (1,), ())
+        h01_grouped = regroup_hidden(h01)
+        quantise_w_bil(2, 0, b20)
+        quantise_hidden(0, 1, h01_grouped)
         second_matmul((0, 1), 0, (2,), ())
+        first_matmul(h11, 1, 1, (2, 3))
         second_matmul((0, 1), 0, (3,), ())
+        b21 = regroup_w_bil(2, 1)
+        quantise_w_bil(2, 1, b21)
+        h11_grouped = regroup_hidden(h11)
+        quantise_hidden(1, 1, h11_grouped)
         b30 = regroup_w_bil(3, 0)
+        second_matmul((2,), 0, (0, 1, 2, 3), ())
         b31 = regroup_w_bil(3, 1)
         quantise_w_bil(3, 0, b30)
         quantise_w_bil(3, 1, b31)
@@ -311,10 +313,7 @@ def tile_bilinearpairedlayer_pa_kernel(tc, x_l, W_l, b_l, W_bil, out):
         second_matmul((0, 1), 1, (1,), ())
         second_matmul((0, 1), 1, (2,), ())
         second_matmul((0, 1), 1, (3,), ())
-        second_matmul((2, 3), 0, (0,), ())
-        second_matmul((2, 3), 0, (1,), ())
-        second_matmul((2, 3), 0, (2,), ())
-        second_matmul((2, 3), 0, (3,), ())
+        second_matmul((3,), 0, (0, 1, 2, 3), ())
         second_matmul((2, 3), 1, (0,), (1,))
         second_matmul((2, 3), 1, (1,), (1,))
         second_matmul((2, 3), 1, (2,), (1,))

@@ -35,6 +35,7 @@ def tile_bilinearpairedlayer_pa_kernel(tc, x_l, W_l, b_l, W_bil, out):
         ctx.enter_context(tc.manual_schedule())
         keep = ctx.enter_context(tc.tile_pool(name="keep", bufs=1))
         w_stage = ctx.enter_context(tc.tile_pool(name="w_stage", bufs=8))
+        o_words = ctx.enter_context(tc.tile_pool(name="o_words", bufs=3))
         h_stage = ctx.enter_context(tc.tile_pool(name="h_stage", bufs=3))
         b_stage = ctx.enter_context(tc.tile_pool(name="b_stage", bufs=4))
         o_stage = ctx.enter_context(tc.tile_pool(name="o_stage", bufs=8))
@@ -97,10 +98,19 @@ def tile_bilinearpairedlayer_pa_kernel(tc, x_l, W_l, b_l, W_bil, out):
         wb_codes = keep.tile([P, ROUNDS, H_PASSES, BANK], U32, name="wb_codes", align_bytes=64)
         wb_scales = keep.tile([P, ROUNDS, H_PASSES, BANK], U8, name="wb_scales", align_bytes=64)
 
-        def transpose_four(words, first_words):
+        def order_words(words):
+            n = words.shape[1]
+            ordered = o_words.tile([P, 2 * WINDOW * WORDS], F32, name="ordered")
+            nc.vector.tensor_copy(
+                out=ordered[:, 0:n].rearrange("p (s u w) -> p s u w", u=2, w=P),
+                in_=words.rearrange("p (s w u) -> p s u w", u=2, w=P),
+            )
+            return ordered
+
+        def transpose_four(words, first_words, step=2):
             bank = psum.tile([P, BANK], F32, tag="bank", name="bank")
             for i, first in enumerate(first_words):
-                nc.tensor.transpose(bank[:, i * P : (i + 1) * P], words[:, first : first + 2 * P - 1 : 2], ident[:])
+                nc.tensor.transpose(bank[:, i * P : (i + 1) * P], words[:, first : first + step * (P - 1) + 1 : step], ident[:])
             return bank[:].rearrange("p (r u a) -> p r a u", r=2, u=2, a=P)
 
         x_words = x_grouped[:].bitcast(F32).rearrange(
@@ -112,11 +122,12 @@ def tile_bilinearpairedlayer_pa_kernel(tc, x_l, W_l, b_l, W_bil, out):
             nc.vector.memset(x_values[:, b, 0, 0, :], 0.0)
             nc.vector.memset(x_values[:, b, LANES + 1, P - 1, :], 0.0)
 
-        def turn_x(b):
-            raw_words = x_raw[b][:].bitcast(F32)
+        def turn_x(b, ordered=None):
+            raw_words = ordered[:] if ordered else x_raw[b][:].bitcast(F32)
+            step, jump = (1, P) if ordered else (2, 1)
             for sp in range(LANES // 2):
-                firsts = [(2 * sp + r) * WORDS + u for r in range(2) for u in range(2)]
-                turned = transpose_four(raw_words, firsts)
+                firsts = [(2 * sp + r) * WORDS + u * jump for r in range(2) for u in range(2)]
+                turned = transpose_four(raw_words, firsts, step)
                 nc.scalar.copy(out=x_words[:, b, 1 + 2 * sp : 3 + 2 * sp, :, :], in_=turned)
 
         def finish_x(b):
@@ -130,12 +141,13 @@ def tile_bilinearpairedlayer_pa_kernel(tc, x_l, W_l, b_l, W_bil, out):
                     in_=x_grouped[:, start : start + cols * PACK],
                 )
 
-        def turn_w_l(g, tp, evacuate):
-            raw_words = wl_raw[(g, tp)][:].rearrange("p r f -> p (r f)").bitcast(F32)
+        def turn_w_l(g, tp, evacuate, ordered=None):
+            raw_words = ordered[:] if ordered else wl_raw[(g, tp)][:].rearrange("p r f -> p (r f)").bitcast(F32)
+            step, jump = (1, P) if ordered else (2, 1)
             parts = []
             for c in range(WINDOW):
-                firsts = [(r * WINDOW + c) * WORDS + u for r in range(2) for u in range(2)]
-                turned = transpose_four(raw_words, firsts)
+                firsts = [(r * WINDOW + c) * WORDS + u * jump for r in range(2) for u in range(2)]
+                turned = transpose_four(raw_words, firsts, step)
                 w_grouped = w_stage.tile([P, 2 * P * PACK], BF16, name="w_grouped", align_bytes=64)
                 target = w_grouped[:].bitcast(F32).rearrange("p (r a u) -> p r a u", r=2, a=P, u=2)
                 if c in evacuate:
@@ -266,9 +278,10 @@ def tile_bilinearpairedlayer_pa_kernel(tc, x_l, W_l, b_l, W_bil, out):
         h00 = new_hidden_rows()
         first_matmul(h00, 0, 0, (0, 1, 2, 3))
         b00 = regroup_w_bil(0, 0)
+        o10 = order_words(wl_raw[(1, 0)][:].rearrange("p r f -> p (r f)").bitcast(F32))
         b10 = regroup_w_bil(1, 0)
         quantise_w_bil(0, 0, b00)
-        w10 = turn_w_l(1, 0, ())
+        w10 = turn_w_l(1, 0, (), o10)
         quantise_w_bil(1, 0, b10)
         quantise_w_l(1, 0, w10)
         h00_grouped = regroup_hidden(h00)

@@ -123,8 +123,8 @@ def tile_bilinearpairedlayer_pa_kernel(tc, x_l, W_l, b_l, W_bil, out):
             nc.vector.memset(x_values[:, b, LANES + 1, P - 1, :], 0.0)
 
         def turn_x(b, ordered=None):
-            raw_words = ordered[:] if ordered else x_raw[b][:].bitcast(F32)
-            step, jump = (1, P) if ordered else (2, 1)
+            raw_words = ordered[:] if ordered is not None else x_raw[b][:].bitcast(F32)
+            step, jump = (1, P) if ordered is not None else (2, 1)
             for sp in range(LANES // 2):
                 firsts = [(2 * sp + r) * WORDS + u * jump for r in range(2) for u in range(2)]
                 turned = transpose_four(raw_words, firsts, step)
@@ -142,8 +142,8 @@ def tile_bilinearpairedlayer_pa_kernel(tc, x_l, W_l, b_l, W_bil, out):
                 )
 
         def turn_w_l(g, tp, evacuate, ordered=None):
-            raw_words = ordered[:] if ordered else wl_raw[(g, tp)][:].rearrange("p r f -> p (r f)").bitcast(F32)
-            step, jump = (1, P) if ordered else (2, 1)
+            raw_words = ordered[:] if ordered is not None else wl_raw[(g, tp)][:].rearrange("p r f -> p (r f)").bitcast(F32)
+            step, jump = (1, P) if ordered is not None else (2, 1)
             parts = []
             for c in range(WINDOW):
                 firsts = [(r * WINDOW + c) * WORDS + u * jump for r in range(2) for u in range(2)]
@@ -272,50 +272,50 @@ def tile_bilinearpairedlayer_pa_kernel(tc, x_l, W_l, b_l, W_bil, out):
         turn_x(0)
         finish_x(0)
         w00 = turn_w_l(0, 0, ())
-        quantise_w_l(0, 0, w00)
         w01 = turn_w_l(0, 1, ())
+        quantise_w_l(0, 0, w00)
         quantise_w_l(0, 1, w01)
-        h00 = new_hidden_rows()
-        first_matmul(h00, 0, 0, (0, 1, 2, 3))
         b00 = regroup_w_bil(0, 0)
         o10 = order_words(wl_raw[(1, 0)][:].rearrange("p r f -> p (r f)").bitcast(F32))
-        b10 = regroup_w_bil(1, 0)
+        o11 = order_words(wl_raw[(1, 1)][:].rearrange("p r f -> p (r f)").bitcast(F32))
         quantise_w_bil(0, 0, b00)
-        w10 = turn_w_l(1, 0, (), o10)
-        quantise_w_bil(1, 0, b10)
+        h00 = new_hidden_rows()
+        first_matmul(h00, 0, 0, (0, 1, 2, 3))
+        w10 = turn_w_l(1, 0, (1,), o10)
         quantise_w_l(1, 0, w10)
-        h00_grouped = regroup_hidden(h00)
-        w11 = turn_w_l(1, 1, ())
-        quantise_hidden(0, 0, h00_grouped)
+        b10 = regroup_w_bil(1, 0)
+        w11 = turn_w_l(1, 1, (), o11)
         turn_x(1)
-        quantise_w_l(1, 1, w11)
-        finish_x(1)
         b11 = new_pieces()
         regroup_w_bil_on_scalar(b11, 1, 1, 0)
+        quantise_w_l(1, 1, w11)
+        finish_x(1)
+        b01 = regroup_w_bil(0, 1)
+        h00_grouped = regroup_hidden(h00)
         h10 = new_hidden_rows()
         first_matmul(h10, 1, 0, (0, 1, 2, 3))
-        b01 = regroup_w_bil(0, 1)
+        quantise_w_bil(0, 1, b01)
+        quantise_hidden(0, 0, h00_grouped)
+        h10_grouped = regroup_hidden(h10)
         regroup_w_bil_on_scalar(b11, 1, 1, 1)
         h01 = new_hidden_rows()
         first_matmul(h01, 0, 1, (0, 1, 2, 3))
-        h10_grouped = regroup_hidden(h10)
-        quantise_w_bil(0, 1, b01)
+        quantise_w_bil(1, 0, b10)
         quantise_hidden(1, 0, h10_grouped)
         quantise_w_bil(1, 1, b11)
         b20 = regroup_w_bil(2, 0)
-        h11 = new_hidden_rows()
-        first_matmul(h11, 1, 1, (0, 1))
-        second_matmul((0, 1), 0, (0,), ())
-        second_matmul((0, 1), 0, (1,), ())
         h01_grouped = regroup_hidden(h01)
+        b21 = regroup_w_bil(2, 1)
+        h11 = new_hidden_rows()
+        first_matmul(h11, 1, 1, (0, 1, 2, 3))
         quantise_w_bil(2, 0, b20)
         quantise_hidden(0, 1, h01_grouped)
-        second_matmul((0, 1), 0, (2,), ())
-        first_matmul(h11, 1, 1, (2, 3))
-        second_matmul((0, 1), 0, (3,), ())
-        b21 = regroup_w_bil(2, 1)
         quantise_w_bil(2, 1, b21)
         h11_grouped = regroup_hidden(h11)
+        second_matmul((0, 1), 0, (0,), ())
+        second_matmul((0, 1), 0, (1,), ())
+        second_matmul((0, 1), 0, (2,), ())
+        second_matmul((0, 1), 0, (3,), ())
         quantise_hidden(1, 1, h11_grouped)
         b30 = regroup_w_bil(3, 0)
         second_matmul((2,), 0, (0, 1, 2, 3), ())

from contextlib import ExitStack

import concourse.mybir as mybir
from concourse.masks import make_identity

F32 = mybir.dt.float32
BF16 = mybir.dt.bfloat16
U32 = mybir.dt.uint32
U8 = mybir.dt.uint8
FP8X4 = mybir.dt.float8_e4m3fn_x4
RELU = mybir.ActivationFunctionType.Relu

P = 128
PACK = 4
K_PASS = P * PACK
BANK = 512

SEQS, POSITIONS, FEATURES, WINDOW, HIDDEN, MAPS = 2, 512, 512, 3, 1024, 2
H_PASSES = HIDDEN // K_PASS
H_TILES = HIDDEN // P
LANES = POSITIONS // P
X_BLOCKS = LANES + 2
X_COLS = X_BLOCKS * P
WORDS = FEATURES // 2
ROUNDS = MAPS * HIDDEN // BANK
TOKEN_TILES = SEQS * LANES
SHIFTS = (0, -1, 1)

FLOPS = 2 * SEQS * POSITIONS * HIDDEN * (WINDOW * FEATURES + MAPS * HIDDEN)


def tile_bilinearpairedlayer_pa_kernel(tc, x_l, W_l, b_l, W_bil, out):
    nc = tc.nc
    with ExitStack() as ctx:
        ctx.enter_context(tc.manual_schedule())
        keep = ctx.enter_context(tc.tile_pool(name="keep", bufs=1))
        w_stage = ctx.enter_context(tc.tile_pool(name="w_stage", bufs=8))
        o_words = ctx.enter_context(tc.tile_pool(name="o_words", bufs=3))
        h_stage = ctx.enter_context(tc.tile_pool(name="h_stage", bufs=3))
        b_stage = ctx.enter_context(tc.tile_pool(name="b_stage", bufs=4))
        o_stage = ctx.enter_context(tc.tile_pool(name="o_stage", bufs=8))
        psum = ctx.enter_context(tc.psum_pool(name="psum", bufs=8))

        wl_view = W_l.rearrange("(g p tp t2) f -> g tp p t2 f", g=H_PASSES, p=P, tp=2, t2=2)
        x_raw = {}
        wl_raw = {}
        wb_raw = {}

        def load_x(b, parts=1):
            x_tile = keep.tile([P, LANES * FEATURES], BF16, name="x_raw%d" % b)
            view = x_l[b].rearrange("(a s) f -> a (s f)", s=LANES)
            n = LANES * FEATURES // parts
            for i in range(parts):
                nc.sync.dma_start(out=x_tile[:, i * n : (i + 1) * n], in_=view[:, i * n : (i + 1) * n])
            x_raw[b] = x_tile

        bias_bf = keep.tile([P, H_TILES], BF16, name="bias_bf")
        nc.scalar.dma_start(
            out=bias_bf[:].rearrange("p (g t) -> p g t", g=H_PASSES),
            in_=b_l.rearrange("(g p t) -> p g t", g=H_PASSES, p=P, t=PACK),
        )

        def load_w_l(g, tp, cuts=(0, WINDOW)):
            wl_tile = keep.tile([P, 2, WINDOW * FEATURES], BF16, name="wl_raw%d%d" % (g, tp))
            for first, last in zip(cuts, cuts[1:]):
                cols = slice(first * FEATURES, last * FEATURES)
                nc.sync.dma_start(out=wl_tile[:, :, cols], in_=wl_view[g, tp][:, :, cols])
            wl_raw[(g, tp)] = wl_tile

        def load_w_bil(k, g):
            wb_tile = keep.tile([P, PACK, HIDDEN], BF16, name="wb_raw%d%d" % (k, g))
            nc.sync.dma_start(
                out=wb_tile[:],
                in_=W_bil[k, g * K_PASS : (g + 1) * K_PASS, :].rearrange("(p t) n -> p t n", t=PACK),
            )
            wb_raw[(k, g)] = wb_tile

        load_x(0)
        load_w_l(0, 0)
        load_w_l(0, 1)
        load_w_bil(0, 0)
        load_w_l(1, 0)
        load_w_l(1, 1)
        load_x(1)
        load_w_bil(0, 1)
        load_w_bil(1, 0)
        load_w_bil(1, 1)
        ident = keep.tile([P, P], F32, name="ident")
        make_identity(nc, ident[:])

        x_grouped = keep.tile([P, SEQS * X_COLS * PACK], BF16, name="x_grouped", align_bytes=64)
        x_codes = keep.tile([P, SEQS, X_COLS], U32, name="x_codes", align_bytes=64)
        x_scales = keep.tile([P, SEQS, X_COLS], U8, name="x_scales", align_bytes=64)
        wl_codes = keep.tile([P, WINDOW, HIDDEN], U32, name="wl_codes", align_bytes=64)
        wl_scales = keep.tile([P, WINDOW, HIDDEN], U8, name="wl_scales", align_bytes=64)
        hl_codes = keep.tile([P, H_PASSES, SEQS * POSITIONS], U32, name="hl_codes", align_bytes=64)
        hl_scales = keep.tile([P, H_PASSES, SEQS * POSITIONS], U8, name="hl_scales", align_bytes=64)
        wb_codes = keep.tile([P, ROUNDS, H_PASSES, BANK], U32, name="wb_codes", align_bytes=64)
        wb_scales = keep.tile([P, ROUNDS, H_PASSES, BANK], U8, name="wb_scales", align_bytes=64)

        def order_words(words):
            n = words.shape[1]
            ordered = o_words.tile([P, 2 * WINDOW * WORDS], F32, name="ordered")
            nc.vector.tensor_copy(
                out=ordered[:, 0:n].rearrange("p (s u w) -> p s u w", u=2, w=P),
                in_=words.rearrange("p (s w u) -> p s u w", u=2, w=P),
            )
            return ordered

        def transpose_four(words, first_words, step=2):
            bank = psum.tile([P, BANK], F32, tag="bank", name="bank")
            for i, first in enumerate(first_words):
                nc.tensor.transpose(bank[:, i * P : (i + 1) * P], words[:, first : first + step * (P - 1) + 1 : step], ident[:])
            return bank[:].rearrange("p (r u a) -> p r a u", r=2, u=2, a=P)

        x_words = x_grouped[:].bitcast(F32).rearrange(
            "p (b j a u) -> p b j a u", b=SEQS, j=X_BLOCKS, a=P, u=2
        )
        x_values = x_grouped[:].rearrange("p (b j a t) -> p b j a t", b=SEQS, j=X_BLOCKS, a=P, t=PACK)

        for b in range(SEQS):
            nc.vector.memset(x_values[:, b, 0, 0, :], 0.0)
            nc.vector.memset(x_values[:, b, LANES + 1, P - 1, :], 0.0)

        def turn_x(b, ordered=None):
            raw_words = ordered[:] if ordered is not None else x_raw[b][:].bitcast(F32)
            step, jump = (1, P) if ordered is not None else (2, 1)
            for sp in range(LANES // 2):
                firsts = [(2 * sp + r) * WORDS + u * jump for r in range(2) for u in range(2)]
                turned = transpose_four(raw_words, firsts, step)
                nc.scalar.copy(out=x_words[:, b, 1 + 2 * sp : 3 + 2 * sp, :, :], in_=turned)

        def finish_x(b):
            nc.vector.tensor_copy(out=x_values[:, b, LANES + 1, 0 : P - 1, :], in_=x_values[:, b, 1, 1:P, :])
            nc.vector.tensor_copy(out=x_values[:, b, 0, 1:P, :], in_=x_values[:, b, LANES, 0 : P - 1, :])
            for first, cols in ((P, 4 * P), (0, P), (5 * P, P)):
                start = (b * X_COLS + first) * PACK
                nc.vector.quantize_mx(
                    out=x_codes[:, b, first : first + cols].bitcast(FP8X4),
                    scales=x_scales[:, b, first : first + cols],
                    in_=x_grouped[:, start : start + cols * PACK],
                )

        def turn_w_l(g, tp, evacuate, ordered=None):
            raw_words = ordered[:] if ordered is not None else wl_raw[(g, tp)][:].rearrange("p r f -> p (r f)").bitcast(F32)
            step, jump = (1, P) if ordered is not None else (2, 1)
            parts = []
            for c in range(WINDOW):
                firsts = [(r * WINDOW + c) * WORDS + u * jump for r in range(2) for u in range(2)]
                turned = transpose_four(raw_words, firsts, step)
                w_grouped = w_stage.tile([P, 2 * P * PACK], BF16, name="w_grouped", align_bytes=64)
                target = w_grouped[:].bitcast(F32).rearrange("p (r a u) -> p r a u", r=2, a=P, u=2)
                if c in evacuate:
                    nc.vector.tensor_copy(out=target, in_=turned)
                else:
                    nc.scalar.copy(out=target, in_=turned)
                parts.append(w_grouped)
            return parts

        def quantise_w_l(g, tp, parts):
            cols = slice((2 * g + tp) * 2 * P, (2 * g + tp + 1) * 2 * P)
            for c in range(WINDOW):
                nc.vector.quantize_mx(
                    out=wl_codes[:, c, cols].bitcast(FP8X4),
                    scales=wl_scales[:, c, cols],
                    in_=parts[c][:],
                )

        def regroup(grouped, rows):
            nc.vector.tensor_copy(
                out=grouped.rearrange("p (c i) t -> p c t i", i=4),
                in_=rows.rearrange("p t (c i) -> p c t i", i=4),
            )

        def new_pieces():
            b_grouped = b_stage.tile([P, BANK, PACK], BF16, name="b_grouped", align_bytes=64)
            return b_grouped

        def regroup_w_bil_on_scalar(b_grouped, rnd, g, part):
            k, half = divmod(rnd, HIDDEN // BANK)
            cols = slice(part * BANK // 2, (part + 1) * BANK // 2)
            raw = slice(half * BANK + part * BANK // 2, half * BANK + (part + 1) * BANK // 2)
            nc.scalar.copy(
                out=b_grouped[:, cols, :].rearrange("p (c i) t -> p c t i", i=4),
                in_=wb_raw[(k, g)][:, :, raw].rearrange("p t (c i) -> p c t i", i=4),
            )

        def regroup_w_bil(rnd, g):
            k, half = divmod(rnd, HIDDEN // BANK)
            b_grouped = b_stage.tile([P, BANK, PACK], BF16, name="b_grouped", align_bytes=64)
            regroup(b_grouped[:], wb_raw[(k, g)][:, :, half * BANK : (half + 1) * BANK])
            return b_grouped

        def quantise_w_bil(rnd, g, b_grouped):
            nc.vector.quantize_mx(
                out=wb_codes[:, rnd, g, :].bitcast(FP8X4),
                scales=wb_scales[:, rnd, g, :],
                in_=b_grouped[:].rearrange("p n t -> p (n t)"),
            )

        def first_matmul(h_rows, g, b, ts):
            for t in ts:
                h_tile = g * PACK + t
                acc = psum.tile([P, BANK], F32, tag="bank", name="acc")
                for c in range(WINDOW):
                    first = (1 + SHIFTS[c]) * P
                    nc.tensor.matmul_mx(
                        out=acc[:],
                        lhsT=wl_codes[:, c, h_tile * P : (h_tile + 1) * P].bitcast(FP8X4),
                        lhsT_scale=wl_scales[:, c, h_tile * P : (h_tile + 1) * P],
                        rhs=x_codes[:, b, first : first + POSITIONS].bitcast(FP8X4),
                        rhs_scale=x_scales[:, b, first : first + POSITIONS],
                        start=(c == 0),
                        stop=(c == WINDOW - 1),
                    )
                nc.scalar.activation(
                    out=h_rows[:, t, :], in_=acc[:], func=RELU, bias=bias_bf[:, h_tile : h_tile + 1], scale=1.0
                )

        def new_hidden_rows():
            h_rows = h_stage.tile([P, PACK, POSITIONS], BF16, name="h_rows")
            return h_rows

        def regroup_hidden(h_rows):
            h_grouped = h_stage.tile([P, POSITIONS, PACK], BF16, name="h_grouped", align_bytes=64)
            regroup(h_grouped[:], h_rows[:])
            return h_grouped

        def quantise_hidden(g, b, h_grouped):
            nc.vector.quantize_mx(
                out=hl_codes[:, g, b * POSITIONS : (b + 1) * POSITIONS].bitcast(FP8X4),
                scales=hl_scales[:, g, b * POSITIONS : (b + 1) * POSITIONS],
                in_=h_grouped[:].rearrange("p n t -> p (n t)"),
            )

        out_view = out.rearrange("b (a s) k n -> b s a k n", s=LANES)

        def fill_bank(rnd, m):
            acc = psum.tile([P, BANK], F32, tag="bank", name="acc")
            for g in range(H_PASSES):
                nc.tensor.matmul_mx(
                    out=acc[:],
                    lhsT=hl_codes[:, g, m * P : (m + 1) * P].bitcast(FP8X4),
                    lhsT_scale=hl_scales[:, g, m * P : (m + 1) * P],
                    rhs=wb_codes[:, rnd, g, :].bitcast(FP8X4),
                    rhs_scale=wb_scales[:, rnd, g, :],
                    start=(g == 0),
                    stop=(g == H_PASSES - 1),
                )
            return acc

        def second_matmul(rnds, b, lanes, vector_banks, whole=True):
            k, half = divmod(rnds[0], HIDDEN // BANK)
            for i, s in enumerate(lanes):
                m = b * LANES + s
                result = o_stage.tile([P, 2 * BANK], F32, name="result")
                for j, rnd in enumerate(rnds):
                    acc = fill_bank(rnd, m)
                    target = result[:, j * BANK : (j + 1) * BANK]
                    if i * len(rnds) + j in vector_banks:
                        nc.vector.tensor_copy(out=target, in_=acc[:])
                    else:
                        nc.scalar.copy(out=target, in_=acc[:])
                    if not whole:
                        nc.sync.dma_start(out=out_view[b, s][:, k, (half + j) * BANK : (half + j + 1) * BANK], in_=target)
                if whole:
                    nc.sync.dma_start(
                        out=out_view[b, s][:, k, half * BANK : half * BANK + len(rnds) * BANK],
                        in_=result[:, 0 : len(rnds) * BANK],
                    )

        turn_x(0)
        finish_x(0)
        w00 = turn_w_l(0, 0, ())
        w01 = turn_w_l(0, 1, ())
        quantise_w_l(0, 0, w00)
        quantise_w_l(0, 1, w01)
        b00 = regroup_w_bil(0, 0)
        o10 = order_words(wl_raw[(1, 0)][:].rearrange("p r f -> p (r f)").bitcast(F32))
        o11 = order_words(wl_raw[(1, 1)][:].rearrange("p r f -> p (r f)").bitcast(F32))
        quantise_w_bil(0, 0, b00)
        h00 = new_hidden_rows()
        first_matmul(h00, 0, 0, (0, 1, 2, 3))
        w10 = turn_w_l(1, 0, (1,), o10)
        quantise_w_l(1, 0, w10)
        b10 = regroup_w_bil(1, 0)
        w11 = turn_w_l(1, 1, (), o11)
        turn_x(1)
        b11 = new_pieces()
        regroup_w_bil_on_scalar(b11, 1, 1, 0)
        quantise_w_l(1, 1, w11)
        finish_x(1)
        b01 = regroup_w_bil(0, 1)
        h00_grouped = regroup_hidden(h00)
        h10 = new_hidden_rows()
        first_matmul(h10, 1, 0, (0, 1, 2, 3))
        quantise_w_bil(0, 1, b01)
        quantise_hidden(0, 0, h00_grouped)
        h10_grouped = regroup_hidden(h10)
        regroup_w_bil_on_scalar(b11, 1, 1, 1)
        h01 = new_hidden_rows()
        first_matmul(h01, 0, 1, (0, 1, 2, 3))
        quantise_w_bil(1, 0, b10)
        quantise_hidden(1, 0, h10_grouped)
        quantise_w_bil(1, 1, b11)
        b20 = regroup_w_bil(2, 0)
        h01_grouped = regroup_hidden(h01)
        b21 = regroup_w_bil(2, 1)
        h11 = new_hidden_rows()
        first_matmul(h11, 1, 1, (0, 1, 2, 3))
        quantise_w_bil(2, 0, b20)
        quantise_hidden(0, 1, h01_grouped)
        quantise_w_bil(2, 1, b21)
        h11_grouped = regroup_hidden(h11)
        second_matmul((0, 1), 0, (0,), ())
        second_matmul((0, 1), 0, (1,), ())
        second_matmul((0, 1), 0, (2,), ())
        second_matmul((0, 1), 0, (3,), ())
        quantise_hidden(1, 1, h11_grouped)
        b30 = regroup_w_bil(3, 0)
        second_matmul((2,), 0, (0, 1, 2, 3), ())
        b31 = regroup_w_bil(3, 1)
        quantise_w_bil(3, 0, b30)
        quantise_w_bil(3, 1, b31)
        second_matmul((0, 1), 1, (0,), ())
        second_matmul((0, 1), 1, (1,), ())
        second_matmul((0, 1), 1, (2,), ())
        second_matmul((0, 1), 1, (3,), ())
        second_matmul((3,), 0, (0, 1, 2, 3), ())
        second_matmul((2, 3), 1, (0,), (1,))
        second_matmul((2, 3), 1, (1,), (1,))
        second_matmul((2, 3), 1, (2,), (1,))
        second_matmul((2, 3), 1, (3,), (1,))
